import numpy as np
import ml_dtypes


def mxq(x, axis, fmt="e4m3"):
    dtype, down = {"e4m3": (ml_dtypes.float8_e4m3fn, 7), "e5m2": (ml_dtypes.float8_e5m2, 14)}[fmt]
    v = np.moveaxis(np.asarray(x, np.float32).astype(ml_dtypes.bfloat16).astype(np.float64), axis, -1)
    blocks = v.reshape(v.shape[:-1] + (-1, 32))
    amax = np.abs(blocks).max(-1, keepdims=True)
    byte = np.maximum(np.where(amax > 0, np.frexp(amax)[1] - 1 + 127, 0) - down, 1)
    scale = np.exp2(byte - 127.0)
    codes = (blocks / scale).astype(np.float32).astype(dtype).astype(np.float64)
    return np.moveaxis((codes * scale).reshape(v.shape), -1, axis)


WIDE = False


def mx_kscale(k):
    if not WIDE:
        return np.ones(k)
    levels = np.array([10, -10, 5, -5, 0])
    a = np.random.permutation(np.resize(levels, k // 512 * 4)).reshape(k // 512, 4)
    idx = np.arange(k)
    return np.exp2(a[idx // 512, idx % 128 // 32])


BF16 = ml_dtypes.bfloat16


def bf(x):
    return np.asarray(x, np.float32).astype(BF16)


def f64(x):
    return np.asarray(x).astype(np.float64)


E2M1 = np.array([0.0, 0.5, 1.0, 1.5, 2.0, 3.0, 4.0, 6.0, -0.0, -0.5, -1.0, -1.5, -2.0, -3.0, -4.0, -6.0])


def pack_weight(w, fmt):
    k, n = w.shape
    w = f64(bf(w)).reshape(k // 32, 32, n)
    amax = np.abs(w).max(1)
    if fmt == "e4m3":
        byte = np.frexp(amax)[1] - 1 + 127 - 7
    else:
        mant, ex = np.frexp(amax / 6.0)
        byte = np.where(mant > 0.5, ex, ex - 1) + 127
    byte = np.clip(np.where(amax > 0, byte, 1), 1, 254)
    scaled = (w * np.exp2(127.0 - byte)[:, None, :]).reshape(k, n).astype(np.float32)
    by_word = np.ascontiguousarray(scaled.reshape(k // 512, 128, 4, n).transpose(0, 1, 3, 2))
    if fmt == "e4m3":
        words = by_word.astype(ml_dtypes.float8_e4m3fn).view(np.uint8)
    else:
        c = by_word.astype(ml_dtypes.float4_e2m1fn).view(np.uint8) & 0xF
        words = c[..., 0::2] | (c[..., 1::2] << 4)
    return np.ascontiguousarray(words), np.ascontiguousarray(byte.astype(np.uint8).reshape(k // 512, 16, n))


def unpack_weight(words, scales, fmt):
    g, p, n, _ = words.shape
    if fmt == "e4m3":
        vals = np.ascontiguousarray(words).view(ml_dtypes.float8_e4m3fn).astype(np.float64)
    else:
        nib = np.empty((g, p, n, 4), np.uint8)
        nib[..., 0::2] = words & 0xF
        nib[..., 1::2] = words >> 4
        vals = E2M1[nib]
    vals = vals * np.repeat(np.exp2(scales.astype(np.float64) - 127.0), 8, axis=1)[..., None]
    return vals.transpose(0, 1, 3, 2).reshape(g * 512, n)


B, H = 4096, 512
FMT = "e4m3"


def sigmoid(v):
    return 1.0 / (1.0 + np.exp(-v))


def setup_inputs():
    s = mx_kscale(H)
    w = lambda: pack_weight(np.ascontiguousarray((np.random.standard_normal((H, H)) * 0.7 / np.sqrt(H) / s[None, :]).T), FMT)
    b = lambda: bf(np.random.standard_normal(H) * 0.5)
    inputs = bf(np.random.standard_normal((B, H)) * s)
    short_term_memory = bf(np.random.standard_normal((B, H)) * s)
    Wf_words, Wf_scales = w()
    b_f = b()
    Wi_words, Wi_scales = w()
    b_i = b()
    Wg_words, Wg_scales = w()
    b_g = b()
    Wo_words, Wo_scales = w()
    b_o = b()
    return {"inputs": inputs,
            "short_term_memory": short_term_memory,
            "Wf_words": Wf_words, "Wf_scales": Wf_scales, "b_f": b_f,
            "Wi_words": Wi_words, "Wi_scales": Wi_scales, "b_i": b_i,
            "Wg_words": Wg_words, "Wg_scales": Wg_scales, "b_g": b_g,
            "Wo_words": Wo_words, "Wo_scales": Wo_scales, "b_o": b_o}


def reference(inputs, short_term_memory, Wf_words, Wf_scales, b_f, Wi_words, Wi_scales, b_i, Wg_words, Wg_scales, b_g, Wo_words, Wo_scales, b_o):
    z = f64(inputs) + f64(short_term_memory)
    zq = mxq(z, 1, "e4m3")
    c = sigmoid((zq @ unpack_weight(Wf_words, Wf_scales, FMT)) + f64(b_f))
    c = c + sigmoid((zq @ unpack_weight(Wi_words, Wi_scales, FMT)) + f64(b_i)) * np.tanh((zq @ unpack_weight(Wg_words, Wg_scales, FMT)) + f64(b_g))
    h = np.tanh(c) * sigmoid((zq @ unpack_weight(Wo_words, Wo_scales, FMT)) + f64(b_o))
    return np.stack((c, h))

@@ -1,0 +1,283 @@
+from contextlib import ExitStack
+
+import concourse.mybir as mybir
+from concourse.masks import make_identity
+
+F32 = mybir.dt.float32
+BF16 = mybir.dt.bfloat16
+I32 = mybir.dt.int32
+U32 = mybir.dt.uint32
+U8 = mybir.dt.uint8
+FP8X4 = mybir.dt.float8_e4m3fn_x4
+ACT = mybir.ActivationFunctionType
+ALU = mybir.AluOpType
+
+P = 128
+PACK = 4
+QUADRANT = 32
+LIVE_ROWS = 4
+ROWS = 4096
+FEATURES = 512
+GATES = 4
+FORGET = 0
+INPUT = 1
+CANDIDATE = 2
+OUTPUT = 3
+GATE_FUNC = (ACT.Sigmoid, ACT.Sigmoid, ACT.Tanh, ACT.Sigmoid)
+
+GROUP_ROWS = P
+CHUNK_GROUPS = 4
+CHUNK_ROWS = CHUNK_GROUPS * GROUP_ROWS
+CHUNKS = ROWS // CHUNK_ROWS
+GROUPS = ROWS // GROUP_ROWS
+SLICES = FEATURES // P
+ROUNDS = CHUNKS * SLICES
+
+GROUP_LEAD = 6
+CELL_LAG = 1
+HIDDEN_LAG = 2
+
+FLOPS = 2 * ROWS * FEATURES * GATES * FEATURES
+
+
+def tile_lstmcell_pa_t_kernel(
+    tc,
+    inputs,
+    short_term_memory,
+    Wf_words,
+    Wf_scales,
+    b_f,
+    Wi_words,
+    Wi_scales,
+    b_i,
+    Wg_words,
+    Wg_scales,
+    b_g,
+    Wo_words,
+    Wo_scales,
+    b_o,
+    out,
+):
+    nc = tc.nc
+    gate_words = (Wf_words, Wi_words, Wg_words, Wo_words)
+    gate_scales = (Wf_scales, Wi_scales, Wg_scales, Wo_scales)
+    gate_bias = (b_f, b_i, b_g, b_o)
+
+    with ExitStack() as stack:
+        consts = stack.enter_context(tc.tile_pool(name="consts", bufs=1))
+        loads = stack.enter_context(tc.tile_pool(name="loads", bufs=1))
+        prep = stack.enter_context(tc.tile_pool(name="prep", bufs=2))
+        acts = stack.enter_context(tc.tile_pool(name="acts", bufs=3))
+        results = stack.enter_context(tc.tile_pool(name="results", bufs=2))
+        gate_banks = stack.enter_context(tc.psum_pool(name="gate_banks", bufs=1))
+        cell_banks = stack.enter_context(tc.psum_pool(name="cell_banks", bufs=2))
+        turn_banks = stack.enter_context(tc.psum_pool(name="turn_banks", bufs=1))
+        stack.enter_context(tc.manual_schedule())
+
+        x_chunks = []
+        h_chunks = []
+
+        def load_chunk(chunk):
+            rows = slice(chunk * CHUNK_ROWS, (chunk + 1) * CHUNK_ROWS)
+            x_sb = loads.tile([P, CHUNK_GROUPS, FEATURES], BF16, name="x%d" % chunk)
+            h_sb = loads.tile([P, CHUNK_GROUPS, FEATURES], BF16, name="h%d" % chunk)
+            nc.sync.dma_start(out=x_sb[:], in_=inputs[rows, :].rearrange("(g p) k -> p g k", p=P))
+            nc.sync.dma_start(out=h_sb[:], in_=short_term_memory[rows, :].rearrange("(g p) k -> p g k", p=P))
+            x_chunks.append(x_sb)
+            h_chunks.append(h_sb)
+
+        load_chunk(0)
+
+        bias_rows = consts.tile([P, P], BF16)
+        nc.vector.memset(bias_rows[:], 0.0)
+        for gate in range(GATES):
+            nc.scalar.dma_start(
+                out=bias_rows[gate * SLICES : (gate + 1) * SLICES, :],
+                in_=gate_bias[gate].rearrange("(s n) -> s n", n=P),
+            )
+
+        w_words = consts.tile([P, GATES, FEATURES * PACK], U8, align_bytes=64)
+        w_planes = consts.tile([P, GATES, FEATURES], U8, align_bytes=64)
+        nc.vector.memset(w_planes[:].rearrange("p g n -> p (g n)").bitcast(I32), 0)
+        for gate in range(GATES):
+            for r in range(LIVE_ROWS):
+                nc.sync.dma_start(
+                    out=w_planes[r:P:QUADRANT, gate, :].bitcast(I32),
+                    in_=gate_scales[gate][0, r : FEATURES // QUADRANT : LIVE_ROWS, :].bitcast(I32),
+                )
+            nc.sync.dma_start(
+                out=w_words[:, gate, :].bitcast(I32),
+                in_=gate_words[gate][0].rearrange("p n t -> p (n t)").bitcast(I32),
+            )
+        for chunk in range(1, CHUNKS):
+            load_chunk(chunk)
+
+        identity = consts.tile([P, P], F32)
+        make_identity(nc, identity[:])
+
+        bias_rows_f32 = consts.tile([P, P], F32)
+        nc.vector.tensor_copy(out=bias_rows_f32[:], in_=bias_rows[:])
+        bias_turned = turn_banks.tile([P, P], F32, name="bias_turned", tag="z_turned")
+        nc.tensor.transpose(bias_turned[:], bias_rows_f32[:], identity[:])
+        bias_cols = consts.tile([P, GATES * SLICES], F32)
+        nc.vector.tensor_copy(out=bias_cols[:], in_=bias_turned[:, : GATES * SLICES])
+
+        z_rows = {}
+        z_turned = {}
+        z_grouped = {}
+        z_codes = {}
+        z_planes = {}
+
+        def add_group(group):
+            chunk, g = divmod(group, CHUNK_GROUPS)
+            z_rows[group] = prep.tile([P, FEATURES], BF16, name="z_rows")
+            nc.vector.tensor_tensor(
+                out=z_rows[group][:], in0=x_chunks[chunk][:, g, :], in1=h_chunks[chunk][:, g, :], op=ALU.add
+            )
+
+        def turn_group(group):
+            words = z_rows[group][:].bitcast(F32)
+            z_turned[group] = turn_banks.tile([P, 2, GROUP_ROWS], F32, name="z_turned")
+            for u in range(2):
+                nc.tensor.transpose(z_turned[group][:, u, :], words[:, u : FEATURES // 2 : 2], identity[:])
+
+        def regroup_group(group):
+            z_grouped[group] = prep.tile([P, GROUP_ROWS * PACK], BF16, name="z_grouped", align_bytes=64)
+            nc.vector.tensor_copy(
+                out=z_grouped[group][:].bitcast(F32).rearrange("p (r u) -> p r u", u=2),
+                in_=z_turned[group][:].rearrange("p u r -> p r u"),
+            )
+
+        def quantise_group(group):
+            chunk, g = divmod(group, CHUNK_GROUPS)
+            if g == 0:
+                z_codes[chunk] = prep.tile([P, CHUNK_ROWS], U32, name="z_codes", align_bytes=64)
+                z_planes[chunk] = prep.tile([P, CHUNK_ROWS], U8, name="z_planes", align_bytes=64)
+            cols = slice(g * GROUP_ROWS, (g + 1) * GROUP_ROWS)
+            nc.vector.quantize_mx(
+                out=z_codes[chunk][:, cols].bitcast(FP8X4), scales=z_planes[chunk][:, cols], in_=z_grouped[group][:]
+            )
+
+        sums = {}
+        gates = {}
+        products = {}
+        c_turned = {}
+        o_turned = {}
+        tanh_c = {}
+        c_rows = {}
+        h_rows = {}
+
+        def multiply(rnd, gate):
+            chunk, s = divmod(rnd, SLICES)
+            sums[rnd, gate] = gate_banks.tile([P, CHUNK_ROWS], F32, name="sums%d" % gate)
+            nc.tensor.matmul_mx(
+                out=sums[rnd, gate][:],
+                lhsT=w_words[:, gate, s * P * PACK : (s + 1) * P * PACK].bitcast(FP8X4),
+                lhsT_scale=w_planes[:, gate, s * P : (s + 1) * P],
+                rhs=z_codes[chunk][:].bitcast(FP8X4),
+                rhs_scale=z_planes[chunk][:],
+                start=True,
+                stop=True,
+            )
+
+        def activate(rnd, gate):
+            s = rnd % SLICES
+            gates[rnd, gate] = acts.tile([P, CHUNK_ROWS], F32, name="gate%d" % gate)
+            nc.scalar.activation(
+                out=gates[rnd, gate][:],
+                in_=sums[rnd, gate][:],
+                func=GATE_FUNC[gate],
+                bias=bias_cols[:, gate * SLICES + s : gate * SLICES + s + 1],
+                scale=1.0,
+            )
+
+        def gate_candidate(rnd):
+            products[rnd] = acts.tile([P, CHUNK_ROWS], F32, name="product")
+            nc.vector.tensor_tensor(
+                out=products[rnd][:], in0=gates[rnd, INPUT][:], in1=gates[rnd, CANDIDATE][:], op=ALU.mult
+            )
+
+        def turn_cell(rnd):
+            c_turned[rnd] = cell_banks.tile([P, CHUNK_GROUPS, P], F32, name="c_turned")
+            for g in range(CHUNK_GROUPS):
+                cols = slice(g * GROUP_ROWS, (g + 1) * GROUP_ROWS)
+                nc.tensor.matmul(
+                    out=c_turned[rnd][:, g, :],
+                    lhsT=gates[rnd, FORGET][:, cols],
+                    rhs=identity[:],
+                    start=True,
+                    stop=False,
+                    is_transpose=True,
+                )
+                nc.tensor.matmul(
+                    out=c_turned[rnd][:, g, :],
+                    lhsT=products[rnd][:, cols],
+                    rhs=identity[:],
+                    start=False,
+                    stop=True,
+                    is_transpose=True,
+                )
+
+        def store(which, chunk, rows_sb):
+            rows = slice(chunk * CHUNK_ROWS, (chunk + 1) * CHUNK_ROWS)
+            nc.sync.dma_start(out=out[which, rows, :].rearrange("(g p) n -> p g n", p=P), in_=rows_sb[:])
+
+        def copy_cell(rnd):
+            chunk, s = divmod(rnd, SLICES)
+            if s == 0:
+                c_rows[chunk] = results.tile([P, CHUNK_GROUPS, FEATURES], F32, name="c_rows")
+            nc.vector.tensor_copy(out=c_rows[chunk][:, :, s * P : (s + 1) * P], in_=c_turned[rnd][:])
+            if s == SLICES - 1:
+                store(0, chunk, c_rows[chunk])
+
+        def squash_cell(rnd):
+            chunk, s = divmod(rnd, SLICES)
+            tanh_c[rnd] = acts.tile([P, CHUNK_GROUPS, P], F32, name="tanh_c")
+            nc.scalar.activation(out=tanh_c[rnd][:], in_=c_rows[chunk][:, :, s * P : (s + 1) * P], func=ACT.Tanh)
+
+        def turn_output_gate(rnd):
+            o_turned[rnd] = turn_banks.tile([P, CHUNK_GROUPS, P], F32, name="o_turned")
+            for g in range(CHUNK_GROUPS):
+                cols = slice(g * GROUP_ROWS, (g + 1) * GROUP_ROWS)
+                nc.tensor.transpose(o_turned[rnd][:, g, :], gates[rnd, OUTPUT][:, cols], identity[:])
+
+        def form_hidden(rnd):
+            chunk, s = divmod(rnd, SLICES)
+            if s == 0:
+                h_rows[chunk] = results.tile([P, CHUNK_GROUPS, FEATURES], F32, name="h_rows")
+            nc.vector.tensor_tensor(
+                out=h_rows[chunk][:, :, s * P : (s + 1) * P], in0=o_turned[rnd][:], in1=tanh_c[rnd][:], op=ALU.mult
+            )
+            if s == SLICES - 1:
+                store(1, chunk, h_rows[chunk])
+
+        def is_round(rnd):
+            return 0 <= rnd < ROUNDS
+
+        def is_group(group):
+            return 0 <= group < GROUPS
+
+        for it in range(-GROUP_LEAD - 1, ROUNDS + HIDDEN_LAG):
+            if is_round(it - HIDDEN_LAG):
+                turn_output_gate(it - HIDDEN_LAG)
+                form_hidden(it - HIDDEN_LAG)
+            if is_round(it - CELL_LAG):
+                turn_cell(it - CELL_LAG)
+                copy_cell(it - CELL_LAG)
+            group = it + GROUP_LEAD
+            if is_group(group - 1):
+                quantise_group(group - 1)
+            if is_group(group + 1):
+                add_group(group + 1)
+            if is_group(group):
+                turn_group(group)
+                regroup_group(group)
+            for gate in range(GATES):
+                if is_round(it):
+                    activate(it, gate)
+                if is_round(it + 1):
+                    multiply(it + 1, gate)
+            if is_round(it):
+                gate_candidate(it)
+            if is_round(it - CELL_LAG):
+                squash_cell(it - CELL_LAG)

@@ -34,8 +34,11 @@ SLICES = FEATURES // P
 ROUNDS = CHUNKS * SLICES
 
 GROUP_LEAD = 6
-CELL_LAG = 1
-HIDDEN_LAG = 2
+TURN_LAG = 2
+SQUASH_LAG = 3
+HIDDEN_LAG = 4
+GATE_LAG = (TURN_LAG, 0, 0, HIDDEN_LAG)
+SPARE = 2
 
 FLOPS = 2 * ROWS * FEATURES * GATES * FEATURES
 
@@ -67,7 +70,7 @@ def tile_lstmcell_pa_t_kernel(
         consts = stack.enter_context(tc.tile_pool(name="consts", bufs=1))
         loads = stack.enter_context(tc.tile_pool(name="loads", bufs=1))
         prep = stack.enter_context(tc.tile_pool(name="prep", bufs=2))
-        acts = stack.enter_context(tc.tile_pool(name="acts", bufs=3))
+        acts = stack.enter_context(tc.tile_pool(name="acts", bufs=SPARE))
         results = stack.enter_context(tc.tile_pool(name="results", bufs=2))
         gate_banks = stack.enter_context(tc.psum_pool(name="gate_banks", bufs=1))
         cell_banks = stack.enter_context(tc.psum_pool(name="cell_banks", bufs=2))
@@ -182,7 +185,7 @@ def tile_lstmcell_pa_t_kernel(
 
         def activate(rnd, gate):
             s = rnd % SLICES
-            gates[rnd, gate] = acts.tile([P, CHUNK_ROWS], F32, name="gate%d" % gate)
+            gates[rnd, gate] = acts.tile([P, CHUNK_ROWS], F32, name="gate%d" % gate, bufs=GATE_LAG[gate] + SPARE)
             nc.scalar.activation(
                 out=gates[rnd, gate][:],
                 in_=sums[rnd, gate][:],
@@ -192,7 +195,7 @@ def tile_lstmcell_pa_t_kernel(
             )
 
         def gate_candidate(rnd):
-            products[rnd] = acts.tile([P, CHUNK_ROWS], F32, name="product")
+            products[rnd] = acts.tile([P, CHUNK_ROWS], F32, name="product", bufs=TURN_LAG + SPARE)
             nc.vector.tensor_tensor(
                 out=products[rnd][:], in0=gates[rnd, INPUT][:], in1=gates[rnd, CANDIDATE][:], op=ALU.mult
             )
@@ -232,7 +235,7 @@ def tile_lstmcell_pa_t_kernel(
 
         def squash_cell(rnd):
             chunk, s = divmod(rnd, SLICES)
-            tanh_c[rnd] = acts.tile([P, CHUNK_GROUPS, P], F32, name="tanh_c")
+            tanh_c[rnd] = acts.tile([P, CHUNK_GROUPS, P], F32, name="tanh_c", bufs=HIDDEN_LAG - SQUASH_LAG + SPARE)
             nc.scalar.activation(out=tanh_c[rnd][:], in_=c_rows[chunk][:, :, s * P : (s + 1) * P], func=ACT.Tanh)
 
         def turn_output_gate(rnd):
@@ -261,9 +264,9 @@ def tile_lstmcell_pa_t_kernel(
             if is_round(it - HIDDEN_LAG):
                 turn_output_gate(it - HIDDEN_LAG)
                 form_hidden(it - HIDDEN_LAG)
-            if is_round(it - CELL_LAG):
-                turn_cell(it - CELL_LAG)
-                copy_cell(it - CELL_LAG)
+            if is_round(it - TURN_LAG):
+                turn_cell(it - TURN_LAG)
+                copy_cell(it - TURN_LAG)
             group = it + GROUP_LEAD
             if is_group(group - 1):
                 quantise_group(group - 1)
@@ -279,5 +282,5 @@ def tile_lstmcell_pa_t_kernel(
                     multiply(it + 1, gate)
             if is_round(it):
                 gate_candidate(it)
-            if is_round(it - CELL_LAG):
-                squash_cell(it - CELL_LAG)
+            if is_round(it - SQUASH_LAG):
+                squash_cell(it - SQUASH_LAG)

@@ -19,11 +19,11 @@ LIVE_ROWS = 4
 ROWS = 4096
 FEATURES = 512
 GATES = 4
-FORGET = 0
-INPUT = 1
-CANDIDATE = 2
+INPUT = 0
+CANDIDATE = 1
+FORGET = 2
 OUTPUT = 3
-GATE_FUNC = (ACT.Sigmoid, ACT.Sigmoid, ACT.Tanh, ACT.Sigmoid)
+GATE_FUNC = (ACT.Sigmoid, ACT.Tanh, ACT.Sigmoid, ACT.Sigmoid)
 
 GROUP_ROWS = P
 CHUNK_GROUPS = 4
@@ -37,7 +37,7 @@ GROUP_LEAD = 6
 TURN_LAG = 2
 SQUASH_LAG = 3
 HIDDEN_LAG = 4
-GATE_LAG = (TURN_LAG, 0, 0, HIDDEN_LAG)
+GATE_LAG = (0, 0, TURN_LAG, HIDDEN_LAG)
 SPARE = 2
 
 FLOPS = 2 * ROWS * FEATURES * GATES * FEATURES
@@ -62,19 +62,18 @@ def tile_lstmcell_pa_t_kernel(
     out,
 ):
     nc = tc.nc
-    gate_words = (Wf_words, Wi_words, Wg_words, Wo_words)
-    gate_scales = (Wf_scales, Wi_scales, Wg_scales, Wo_scales)
-    gate_bias = (b_f, b_i, b_g, b_o)
+    gate_words = (Wi_words, Wg_words, Wf_words, Wo_words)
+    gate_scales = (Wi_scales, Wg_scales, Wf_scales, Wo_scales)
+    gate_bias = (b_i, b_g, b_f, b_o)
 
     with ExitStack() as stack:
         consts = stack.enter_context(tc.tile_pool(name="consts", bufs=1))
         loads = stack.enter_context(tc.tile_pool(name="loads", bufs=1))
-        prep = stack.enter_context(tc.tile_pool(name="prep", bufs=2))
+        prep = stack.enter_context(tc.tile_pool(name="prep", bufs=3))
         acts = stack.enter_context(tc.tile_pool(name="acts", bufs=SPARE))
-        results = stack.enter_context(tc.tile_pool(name="results", bufs=2))
+        results = stack.enter_context(tc.tile_pool(name="results", bufs=4))
         gate_banks = stack.enter_context(tc.psum_pool(name="gate_banks", bufs=1))
-        cell_banks = stack.enter_context(tc.psum_pool(name="cell_banks", bufs=2))
-        turn_banks = stack.enter_context(tc.psum_pool(name="turn_banks", bufs=1))
+        turn_banks = stack.enter_context(tc.psum_pool(name="turn_banks", bufs=4))
         stack.enter_context(tc.manual_schedule())
 
         x_chunks = []
@@ -120,7 +119,7 @@ def tile_lstmcell_pa_t_kernel(
 
         bias_rows_f32 = consts.tile([P, P], F32)
         nc.vector.tensor_copy(out=bias_rows_f32[:], in_=bias_rows[:])
-        bias_turned = turn_banks.tile([P, P], F32, name="bias_turned", tag="z_turned")
+        bias_turned = turn_banks.tile([P, P], F32, name="bias_turned", tag="turned")
         nc.tensor.transpose(bias_turned[:], bias_rows_f32[:], identity[:])
         bias_cols = consts.tile([P, GATES * SLICES], F32)
         nc.vector.tensor_copy(out=bias_cols[:], in_=bias_turned[:, : GATES * SLICES])
@@ -140,7 +139,7 @@ def tile_lstmcell_pa_t_kernel(
 
         def turn_group(group):
             words = z_rows[group][:].bitcast(F32)
-            z_turned[group] = turn_banks.tile([P, 2, GROUP_ROWS], F32, name="z_turned")
+            z_turned[group] = turn_banks.tile([P, 2, GROUP_ROWS], F32, name="z_turned", tag="turned")
             for u in range(2):
                 nc.tensor.transpose(z_turned[group][:, u, :], words[:, u : FEATURES // 2 : 2], identity[:])
 
@@ -168,7 +167,6 @@ def tile_lstmcell_pa_t_kernel(
         o_turned = {}
         tanh_c = {}
         c_rows = {}
-        h_rows = {}
 
         def multiply(rnd, gate):
             chunk, s = divmod(rnd, SLICES)
@@ -201,7 +199,7 @@ def tile_lstmcell_pa_t_kernel(
             )
 
         def turn_cell(rnd):
-            c_turned[rnd] = cell_banks.tile([P, CHUNK_GROUPS, P], F32, name="c_turned")
+            c_turned[rnd] = turn_banks.tile([P, CHUNK_GROUPS, P], F32, name="c_turned", tag="turned")
             for g in range(CHUNK_GROUPS):
                 cols = slice(g * GROUP_ROWS, (g + 1) * GROUP_ROWS)
                 nc.tensor.matmul(
@@ -221,38 +219,30 @@ def tile_lstmcell_pa_t_kernel(
                     is_transpose=True,
                 )
 
-        def store(which, chunk, rows_sb):
-            rows = slice(chunk * CHUNK_ROWS, (chunk + 1) * CHUNK_ROWS)
-            nc.sync.dma_start(out=out[which, rows, :].rearrange("(g p) n -> p g n", p=P), in_=rows_sb[:])
+        def store(which, rnd, rows_sb):
+            chunk, s = divmod(rnd, SLICES)
+            block = out[which, chunk * CHUNK_ROWS : (chunk + 1) * CHUNK_ROWS, s * P : (s + 1) * P]
+            nc.sync.dma_start(out=block.rearrange("(g p) n -> p g n", p=P), in_=rows_sb[:])
 
         def copy_cell(rnd):
-            chunk, s = divmod(rnd, SLICES)
-            if s == 0:
-                c_rows[chunk] = results.tile([P, CHUNK_GROUPS, FEATURES], F32, name="c_rows")
-            nc.vector.tensor_copy(out=c_rows[chunk][:, :, s * P : (s + 1) * P], in_=c_turned[rnd][:])
-            if s == SLICES - 1:
-                store(0, chunk, c_rows[chunk])
+            c_rows[rnd] = results.tile([P, CHUNK_GROUPS, P], F32, name="c_rows")
+            nc.vector.tensor_copy(out=c_rows[rnd][:], in_=c_turned[rnd][:])
+            store(0, rnd, c_rows[rnd])
 
         def squash_cell(rnd):
-            chunk, s = divmod(rnd, SLICES)
             tanh_c[rnd] = acts.tile([P, CHUNK_GROUPS, P], F32, name="tanh_c", bufs=HIDDEN_LAG - SQUASH_LAG + SPARE)
-            nc.scalar.activation(out=tanh_c[rnd][:], in_=c_rows[chunk][:, :, s * P : (s + 1) * P], func=ACT.Tanh)
+            nc.scalar.activation(out=tanh_c[rnd][:], in_=c_rows[rnd][:], func=ACT.Tanh)
 
         def turn_output_gate(rnd):
-            o_turned[rnd] = turn_banks.tile([P, CHUNK_GROUPS, P], F32, name="o_turned")
+            o_turned[rnd] = turn_banks.tile([P, CHUNK_GROUPS, P], F32, name="o_turned", tag="turned")
             for g in range(CHUNK_GROUPS):
                 cols = slice(g * GROUP_ROWS, (g + 1) * GROUP_ROWS)
                 nc.tensor.transpose(o_turned[rnd][:, g, :], gates[rnd, OUTPUT][:, cols], identity[:])
 
         def form_hidden(rnd):
-            chunk, s = divmod(rnd, SLICES)
-            if s == 0:
-                h_rows[chunk] = results.tile([P, CHUNK_GROUPS, FEATURES], F32, name="h_rows")
-            nc.vector.tensor_tensor(
-                out=h_rows[chunk][:, :, s * P : (s + 1) * P], in0=o_turned[rnd][:], in1=tanh_c[rnd][:], op=ALU.mult
-            )
-            if s == SLICES - 1:
-                store(1, chunk, h_rows[chunk])
+            h_rows = results.tile([P, CHUNK_GROUPS, P], F32, name="h_rows")
+            nc.vector.tensor_tensor(out=h_rows[:], in0=o_turned[rnd][:], in1=tanh_c[rnd][:], op=ALU.mult)
+            store(1, rnd, h_rows)
 
         def is_round(rnd):
             return 0 <= rnd < ROUNDS
@@ -269,18 +259,19 @@ def tile_lstmcell_pa_t_kernel(
                 copy_cell(it - TURN_LAG)
             group = it + GROUP_LEAD
             if is_group(group - 1):
-                quantise_group(group - 1)
+                regroup_group(group - 1)
             if is_group(group + 1):
                 add_group(group + 1)
-            if is_group(group):
-                turn_group(group)
-                regroup_group(group)
             for gate in range(GATES):
                 if is_round(it):
                     activate(it, gate)
                 if is_round(it + 1):
                     multiply(it + 1, gate)
+            if is_group(group):
+                turn_group(group)
             if is_round(it):
                 gate_candidate(it)
+            if is_group(group - 1):
+                quantise_group(group - 1)
             if is_round(it - SQUASH_LAG):
                 squash_cell(it - SQUASH_LAG)

@@ -26,6 +26,7 @@ OUTPUT = 3
 GATE_FUNC = (ACT.Sigmoid, ACT.Tanh, ACT.Sigmoid, ACT.Sigmoid)
 
 GROUP_ROWS = P
+PIECE_GROUPS = 2
 CHUNK_GROUPS = 4
 CHUNK_ROWS = CHUNK_GROUPS * GROUP_ROWS
 CHUNKS = ROWS // CHUNK_ROWS
@@ -36,9 +37,9 @@ ROUNDS = CHUNKS * SLICES
 GROUP_LEAD = 6
 TURN_LAG = 2
 SQUASH_LAG = 3
-HIDDEN_LAG = 4
+HIDDEN_LAG = 5
 GATE_LAG = (0, 0, TURN_LAG, HIDDEN_LAG)
-SPARE = 2
+SPARE = 3
 
 FLOPS = 2 * ROWS * FEATURES * GATES * FEATURES
 
@@ -72,23 +73,10 @@ def tile_lstmcell_pa_t_kernel(
         prep = stack.enter_context(tc.tile_pool(name="prep", bufs=3))
         acts = stack.enter_context(tc.tile_pool(name="acts", bufs=SPARE))
         results = stack.enter_context(tc.tile_pool(name="results", bufs=4))
-        gate_banks = stack.enter_context(tc.psum_pool(name="gate_banks", bufs=1))
-        turn_banks = stack.enter_context(tc.psum_pool(name="turn_banks", bufs=4))
+        sum_banks = stack.enter_context(tc.psum_pool(name="sum_banks", bufs=GATES + 1))
+        turn_banks = stack.enter_context(tc.psum_pool(name="turn_banks", bufs=3))
         stack.enter_context(tc.manual_schedule())
 
-        x_chunks = []
-        h_chunks = []
-
-        def load_chunk(chunk):
-            rows = slice(chunk * CHUNK_ROWS, (chunk + 1) * CHUNK_ROWS)
-            x_sb = loads.tile([P, CHUNK_GROUPS, FEATURES], BF16, name="x%d" % chunk)
-            h_sb = loads.tile([P, CHUNK_GROUPS, FEATURES], BF16, name="h%d" % chunk)
-            nc.sync.dma_start(out=x_sb[:], in_=inputs[rows, :].rearrange("(g p) k -> p g k", p=P))
-            nc.sync.dma_start(out=h_sb[:], in_=short_term_memory[rows, :].rearrange("(g p) k -> p g k", p=P))
-            x_chunks.append(x_sb)
-            h_chunks.append(h_sb)
-
-        load_chunk(0)
 
         bias_rows = consts.tile([P, P], BF16)
         nc.vector.memset(bias_rows[:], 0.0)
@@ -98,10 +86,23 @@ def tile_lstmcell_pa_t_kernel(
                 in_=gate_bias[gate].rearrange("(s n) -> s n", n=P),
             )
 
+        x_pieces = []
+        h_pieces = []
+
+        def load_piece(piece):
+            rows = slice(piece * PIECE_GROUPS * GROUP_ROWS, (piece + 1) * PIECE_GROUPS * GROUP_ROWS)
+            x_sb = loads.tile([P, PIECE_GROUPS, FEATURES], BF16, name="x%d" % piece)
+            h_sb = loads.tile([P, PIECE_GROUPS, FEATURES], BF16, name="h%d" % piece)
+            nc.sync.dma_start(out=x_sb[:], in_=inputs[rows, :].rearrange("(g p) k -> p g k", p=P))
+            nc.sync.dma_start(out=h_sb[:], in_=short_term_memory[rows, :].rearrange("(g p) k -> p g k", p=P))
+            x_pieces.append(x_sb)
+            h_pieces.append(h_sb)
+
         w_words = consts.tile([P, GATES, FEATURES * PACK], U8, align_bytes=64)
         w_planes = consts.tile([P, GATES, FEATURES], U8, align_bytes=64)
         nc.vector.memset(w_planes[:].rearrange("p g n -> p (g n)").bitcast(I32), 0)
-        for gate in range(GATES):
+
+        def load_gate(gate):
             for r in range(LIVE_ROWS):
                 nc.sync.dma_start(
                     out=w_planes[r:P:QUADRANT, gate, :].bitcast(I32),
@@ -111,8 +112,16 @@ def tile_lstmcell_pa_t_kernel(
                 out=w_words[:, gate, :].bitcast(I32),
                 in_=gate_words[gate][0].rearrange("p n t -> p (n t)").bitcast(I32),
             )
-        for chunk in range(1, CHUNKS):
-            load_chunk(chunk)
+
+        first_pieces = CHUNK_GROUPS // PIECE_GROUPS
+        for piece in range(first_pieces):
+            load_piece(piece)
+        load_gate(0)
+        load_piece(first_pieces)
+        for gate in range(1, GATES):
+            load_gate(gate)
+        for piece in range(first_pieces + 1, GROUPS // PIECE_GROUPS):
+            load_piece(piece)
 
         identity = consts.tile([P, P], F32)
         make_identity(nc, identity[:])
@@ -131,10 +140,10 @@ def tile_lstmcell_pa_t_kernel(
         z_planes = {}
 
         def add_group(group):
-            chunk, g = divmod(group, CHUNK_GROUPS)
+            piece, g = divmod(group, PIECE_GROUPS)
             z_rows[group] = prep.tile([P, FEATURES], BF16, name="z_rows")
             nc.vector.tensor_tensor(
-                out=z_rows[group][:], in0=x_chunks[chunk][:, g, :], in1=h_chunks[chunk][:, g, :], op=ALU.add
+                out=z_rows[group][:], in0=x_pieces[piece][:, g, :], in1=h_pieces[piece][:, g, :], op=ALU.add
             )
 
         def turn_group(group):
@@ -170,7 +179,7 @@ def tile_lstmcell_pa_t_kernel(
 
         def multiply(rnd, gate):
             chunk, s = divmod(rnd, SLICES)
-            sums[rnd, gate] = gate_banks.tile([P, CHUNK_ROWS], F32, name="sums%d" % gate)
+            sums[rnd, gate] = sum_banks.tile([P, CHUNK_ROWS], F32, name="sums")
             nc.tensor.matmul_mx(
                 out=sums[rnd, gate][:],
                 lhsT=w_words[:, gate, s * P * PACK : (s + 1) * P * PACK].bitcast(FP8X4),
@@ -251,22 +260,22 @@ def tile_lstmcell_pa_t_kernel(
             return 0 <= group < GROUPS
 
         for it in range(-GROUP_LEAD - 1, ROUNDS + HIDDEN_LAG):
+            group = it + GROUP_LEAD
+            if is_group(group - 1):
+                regroup_group(group - 1)
             if is_round(it - HIDDEN_LAG):
                 turn_output_gate(it - HIDDEN_LAG)
                 form_hidden(it - HIDDEN_LAG)
             if is_round(it - TURN_LAG):
                 turn_cell(it - TURN_LAG)
                 copy_cell(it - TURN_LAG)
-            group = it + GROUP_LEAD
-            if is_group(group - 1):
-                regroup_group(group - 1)
             if is_group(group + 1):
                 add_group(group + 1)
             for gate in range(GATES):
-                if is_round(it):
-                    activate(it, gate)
                 if is_round(it + 1):
                     multiply(it + 1, gate)
+                if is_round(it):
+                    activate(it, gate)
             if is_group(group):
                 turn_group(group)
             if is_round(it):

@@ -116,22 +116,28 @@ def tile_lstmcell_pa_t_kernel(
         first_pieces = CHUNK_GROUPS // PIECE_GROUPS
         for piece in range(first_pieces):
             load_piece(piece)
-        load_gate(0)
-        load_piece(first_pieces)
-        for gate in range(1, GATES):
+        for gate in range(GATES):
             load_gate(gate)
-        for piece in range(first_pieces + 1, GROUPS // PIECE_GROUPS):
+            load_piece(first_pieces + gate)
+        for piece in range(first_pieces + GATES, GROUPS // PIECE_GROUPS):
             load_piece(piece)
 
         identity = consts.tile([P, P], F32)
         make_identity(nc, identity[:])
 
         bias_rows_f32 = consts.tile([P, P], F32)
-        nc.vector.tensor_copy(out=bias_rows_f32[:], in_=bias_rows[:])
-        bias_turned = turn_banks.tile([P, P], F32, name="bias_turned", tag="turned")
-        nc.tensor.transpose(bias_turned[:], bias_rows_f32[:], identity[:])
+        bias_turned = {}
         bias_cols = consts.tile([P, GATES * SLICES], F32)
-        nc.vector.tensor_copy(out=bias_cols[:], in_=bias_turned[:, : GATES * SLICES])
+
+        def turn_bias():
+            nc.vector.tensor_copy(out=bias_rows_f32[:], in_=bias_rows[:])
+            bias_turned[0] = turn_banks.tile([P, P], F32, name="bias_turned", tag="turned")
+            nc.tensor.transpose(bias_turned[0][:], bias_rows_f32[:], identity[:])
+
+        def copy_bias():
+            nc.vector.tensor_copy(out=bias_cols[:], in_=bias_turned[0][:, : GATES * SLICES])
+
+        bias_stages = (turn_bias, copy_bias)
 
         z_rows = {}
         z_turned = {}
@@ -192,7 +198,9 @@ def tile_lstmcell_pa_t_kernel(
 
         def activate(rnd, gate):
             s = rnd % SLICES
-            gates[rnd, gate] = acts.tile([P, CHUNK_ROWS], F32, name="gate%d" % gate, bufs=GATE_LAG[gate] + SPARE)
+            gates[rnd, gate] = acts.tile(
+                [P, CHUNK_ROWS], F32, name="gate%d" % gate, bufs=max(GATE_LAG[gate] + SPARE, SLICES + 1)
+            )
             nc.scalar.activation(
                 out=gates[rnd, gate][:],
                 in_=sums[rnd, gate][:],
@@ -259,28 +267,68 @@ def tile_lstmcell_pa_t_kernel(
         def is_group(group):
             return 0 <= group < GROUPS
 
-        for it in range(-GROUP_LEAD - 1, ROUNDS + HIDDEN_LAG):
+        def prepare(groups, fillers):
+            for it in range(-GROUP_LEAD - 1, 0):
+                group = it + GROUP_LEAD
+                if group - 1 in groups:
+                    regroup_group(group - 1)
+                if group + 1 in groups:
+                    add_group(group + 1)
+                if group in groups:
+                    turn_group(group)
+                if 0 <= group + 1 - groups.stop < len(fillers):
+                    fillers[group + 1 - groups.stop]()
+                if group - 1 in groups:
+                    quantise_group(group - 1)
+
+        order = [(s, gate) for gate in range(GATES) for s in range(SLICES)]
+        order.extend([(rnd, gate) for rnd in range(SLICES, ROUNDS) for gate in range(GATES)])
+
+        def made_in(rnd, gate):
+            return gate if rnd < SLICES else rnd
+
+        def product_at(rnd):
+            return max(rnd, made_in(rnd, CANDIDATE))
+
+        def turn_at(rnd):
+            return max(rnd + TURN_LAG, made_in(rnd, FORGET) + 1)
+
+        def squash_at(rnd):
+            return rnd + SQUASH_LAG
+
+        def hidden_at(rnd):
+            return rnd + HIDDEN_LAG
+
+        def due(stage_at, it):
+            return [rnd for rnd in range(ROUNDS) if stage_at(rnd) == it]
+
+        prepare(range(0, CHUNK_GROUPS), bias_stages)
+        for ahead in range(GATES):
+            multiply(order[ahead][0], order[ahead][1])
+        prepare(range(CHUNK_GROUPS, GROUPS), ())
+
+        for it in range(0, ROUNDS + HIDDEN_LAG):
             group = it + GROUP_LEAD
             if is_group(group - 1):
                 regroup_group(group - 1)
-            if is_round(it - HIDDEN_LAG):
-                turn_output_gate(it - HIDDEN_LAG)
-                form_hidden(it - HIDDEN_LAG)
-            if is_round(it - TURN_LAG):
-                turn_cell(it - TURN_LAG)
-                copy_cell(it - TURN_LAG)
+            for rnd in due(hidden_at, it):
+                turn_output_gate(rnd)
+                form_hidden(rnd)
+            for rnd in due(turn_at, it):
+                turn_cell(rnd)
+                copy_cell(rnd)
             if is_group(group + 1):
                 add_group(group + 1)
-            for gate in range(GATES):
-                if is_round(it + 1):
-                    multiply(it + 1, gate)
-                if is_round(it):
-                    activate(it, gate)
+            for place in range(it * GATES, (it + 1) * GATES):
+                if place + GATES < len(order):
+                    multiply(order[place + GATES][0], order[place + GATES][1])
+                if place < len(order):
+                    activate(order[place][0], order[place][1])
             if is_group(group):
                 turn_group(group)
-            if is_round(it):
-                gate_candidate(it)
+            for rnd in due(product_at, it):
+                gate_candidate(rnd)
             if is_group(group - 1):
                 quantise_group(group - 1)
-            if is_round(it - SQUASH_LAG):
-                squash_cell(it - SQUASH_LAG)
+            for rnd in due(squash_at, it):
+                squash_cell(rnd)

@@ -178,6 +178,7 @@ def tile_lstmcell_pa_t_kernel(
         sums = {}
         gates = {}
         products = {}
+        cells = {}
         c_turned = {}
         o_turned = {}
         tanh_c = {}
@@ -215,26 +216,15 @@ def tile_lstmcell_pa_t_kernel(
                 out=products[rnd][:], in0=gates[rnd, INPUT][:], in1=gates[rnd, CANDIDATE][:], op=ALU.mult
             )
 
+        def sum_cell(rnd):
+            cells[rnd] = acts.tile([P, CHUNK_ROWS], F32, name="cell", bufs=TURN_LAG + SPARE)
+            nc.gpsimd.tensor_tensor(out=cells[rnd][:], in0=gates[rnd, FORGET][:], in1=products[rnd][:], op=ALU.add)
+
         def turn_cell(rnd):
             c_turned[rnd] = turn_banks.tile([P, CHUNK_GROUPS, P], F32, name="c_turned", tag="turned")
             for g in range(CHUNK_GROUPS):
                 cols = slice(g * GROUP_ROWS, (g + 1) * GROUP_ROWS)
-                nc.tensor.matmul(
-                    out=c_turned[rnd][:, g, :],
-                    lhsT=gates[rnd, FORGET][:, cols],
-                    rhs=identity[:],
-                    start=True,
-                    stop=False,
-                    is_transpose=True,
-                )
-                nc.tensor.matmul(
-                    out=c_turned[rnd][:, g, :],
-                    lhsT=products[rnd][:, cols],
-                    rhs=identity[:],
-                    start=False,
-                    stop=True,
-                    is_transpose=True,
-                )
+                nc.tensor.transpose(c_turned[rnd][:, g, :], cells[rnd][:, cols], identity[:])
 
         def store(which, rnd, rows_sb):
             chunk, s = divmod(rnd, SLICES)
@@ -290,6 +280,9 @@ def tile_lstmcell_pa_t_kernel(
         def product_at(rnd):
             return max(rnd, made_in(rnd, CANDIDATE))
 
+        def sum_at(rnd):
+            return max(product_at(rnd), made_in(rnd, FORGET))
+
         def turn_at(rnd):
             return max(rnd + TURN_LAG, made_in(rnd, FORGET) + 1)
 
@@ -319,6 +312,8 @@ def tile_lstmcell_pa_t_kernel(
                 copy_cell(rnd)
             if is_group(group + 1):
                 add_group(group + 1)
+            if is_group(group - 1):
+                quantise_group(group - 1)
             for place in range(it * GATES, (it + 1) * GATES):
                 if place + GATES < len(order):
                     multiply(order[place + GATES][0], order[place + GATES][1])
@@ -328,7 +323,7 @@ def tile_lstmcell_pa_t_kernel(
                 turn_group(group)
             for rnd in due(product_at, it):
                 gate_candidate(rnd)
-            if is_group(group - 1):
-                quantise_group(group - 1)
+            for rnd in due(sum_at, it):
+                sum_cell(rnd)
             for rnd in due(squash_at, it):
                 squash_cell(rnd)

@@ -224,7 +224,25 @@ def tile_lstmcell_pa_t_kernel(
             c_turned[rnd] = turn_banks.tile([P, CHUNK_GROUPS, P], F32, name="c_turned", tag="turned")
             for g in range(CHUNK_GROUPS):
                 cols = slice(g * GROUP_ROWS, (g + 1) * GROUP_ROWS)
-                nc.tensor.transpose(c_turned[rnd][:, g, :], cells[rnd][:, cols], identity[:])
+                if rnd in cells:
+                    nc.tensor.transpose(c_turned[rnd][:, g, :], cells[rnd][:, cols], identity[:])
+                else:
+                    nc.tensor.matmul(
+                        out=c_turned[rnd][:, g, :],
+                        lhsT=gates[rnd, FORGET][:, cols],
+                        rhs=identity[:],
+                        start=True,
+                        stop=False,
+                        is_transpose=True,
+                    )
+                    nc.tensor.matmul(
+                        out=c_turned[rnd][:, g, :],
+                        lhsT=products[rnd][:, cols],
+                        rhs=identity[:],
+                        start=False,
+                        stop=True,
+                        is_transpose=True,
+                    )
 
         def store(which, rnd, rows_sb):
             chunk, s = divmod(rnd, SLICES)
@@ -304,12 +322,12 @@ def tile_lstmcell_pa_t_kernel(
             group = it + GROUP_LEAD
             if is_group(group - 1):
                 regroup_group(group - 1)
-            for rnd in due(hidden_at, it):
-                turn_output_gate(rnd)
-                form_hidden(rnd)
             for rnd in due(turn_at, it):
                 turn_cell(rnd)
                 copy_cell(rnd)
+            for rnd in due(hidden_at, it):
+                turn_output_gate(rnd)
+                form_hidden(rnd)
             if is_group(group + 1):
                 add_group(group + 1)
             if is_group(group - 1):
@@ -324,6 +342,7 @@ def tile_lstmcell_pa_t_kernel(
             for rnd in due(product_at, it):
                 gate_candidate(rnd)
             for rnd in due(sum_at, it):
-                sum_cell(rnd)
+                if rnd < ROUNDS - 1:
+                    sum_cell(rnd)
             for rnd in due(squash_at, it):
                 squash_cell(rnd)

@@ -80,11 +80,13 @@ def tile_lstmcell_pa_t_kernel(
 
         bias_rows = consts.tile([P, P], BF16)
         nc.vector.memset(bias_rows[:], 0.0)
-        for gate in range(GATES):
-            nc.scalar.dma_start(
-                out=bias_rows[gate * SLICES : (gate + 1) * SLICES, :],
-                in_=gate_bias[gate].rearrange("(s n) -> s n", n=P),
-            )
+
+        def load_biases():
+            for gate in range(GATES):
+                nc.sync.dma_start(
+                    out=bias_rows[gate * SLICES : (gate + 1) * SLICES, :],
+                    in_=gate_bias[gate].rearrange("(s n) -> s n", n=P),
+                )
 
         x_pieces = []
         h_pieces = []
@@ -114,7 +116,9 @@ def tile_lstmcell_pa_t_kernel(
             )
 
         first_pieces = CHUNK_GROUPS // PIECE_GROUPS
-        for piece in range(first_pieces):
+        load_piece(0)
+        load_biases()
+        for piece in range(1, first_pieces):
             load_piece(piece)
         for gate in range(GATES):
             load_gate(gate)

@@ -33,6 +33,7 @@ CHUNKS = ROWS // CHUNK_ROWS
 GROUPS = ROWS // GROUP_ROWS
 SLICES = FEATURES // P
 ROUNDS = CHUNKS * SLICES
+LAST_ROUND = ROUNDS - 1
 
 GROUP_LEAD = 6
 TURN_LAG = 2
@@ -72,7 +73,7 @@ def tile_lstmcell_pa_t_kernel(
         loads = stack.enter_context(tc.tile_pool(name="loads", bufs=1))
         prep = stack.enter_context(tc.tile_pool(name="prep", bufs=3))
         acts = stack.enter_context(tc.tile_pool(name="acts", bufs=SPARE))
-        results = stack.enter_context(tc.tile_pool(name="results", bufs=4))
+        results = stack.enter_context(tc.tile_pool(name="results", bufs=6))
         sum_banks = stack.enter_context(tc.psum_pool(name="sum_banks", bufs=GATES + 1))
         turn_banks = stack.enter_context(tc.psum_pool(name="turn_banks", bufs=3))
         stack.enter_context(tc.manual_schedule())
@@ -225,7 +226,10 @@ def tile_lstmcell_pa_t_kernel(
             nc.gpsimd.tensor_tensor(out=cells[rnd][:], in0=gates[rnd, FORGET][:], in1=products[rnd][:], op=ALU.add)
 
         def turn_cell(rnd):
-            c_turned[rnd] = turn_banks.tile([P, CHUNK_GROUPS, P], F32, name="c_turned", tag="turned")
+            if rnd == LAST_ROUND:
+                c_turned[rnd] = sum_banks.tile([P, CHUNK_GROUPS, P], F32, name="sums")
+            else:
+                c_turned[rnd] = turn_banks.tile([P, CHUNK_GROUPS, P], F32, name="c_turned", tag="turned")
             for g in range(CHUNK_GROUPS):
                 cols = slice(g * GROUP_ROWS, (g + 1) * GROUP_ROWS)
                 if rnd in cells:
@@ -255,12 +259,14 @@ def tile_lstmcell_pa_t_kernel(
 
         def copy_cell(rnd):
             c_rows[rnd] = results.tile([P, CHUNK_GROUPS, P], F32, name="c_rows")
-            nc.vector.tensor_copy(out=c_rows[rnd][:], in_=c_turned[rnd][:])
+            copy = nc.scalar.copy if rnd == LAST_ROUND else nc.vector.tensor_copy
+            copy(out=c_rows[rnd][:], in_=c_turned[rnd][:])
             store(0, rnd, c_rows[rnd])
 
         def squash_cell(rnd):
             tanh_c[rnd] = acts.tile([P, CHUNK_GROUPS, P], F32, name="tanh_c", bufs=HIDDEN_LAG - SQUASH_LAG + SPARE)
-            nc.scalar.activation(out=tanh_c[rnd][:], in_=c_rows[rnd][:], func=ACT.Tanh)
+            source = c_turned[rnd] if rnd == LAST_ROUND else c_rows[rnd]
+            nc.scalar.activation(out=tanh_c[rnd][:], in_=source[:], func=ACT.Tanh)
 
         def turn_output_gate(rnd):
             o_turned[rnd] = turn_banks.tile([P, CHUNK_GROUPS, P], F32, name="o_turned", tag="turned")
@@ -312,7 +318,8 @@ def tile_lstmcell_pa_t_kernel(
             return rnd + SQUASH_LAG
 
         def hidden_at(rnd):
-            return rnd + HIDDEN_LAG
+            last_quantising = GROUPS - GROUP_LEAD
+            return rnd + HIDDEN_LAG if rnd + HIDDEN_LAG <= last_quantising + 1 else rnd + HIDDEN_LAG - 1
 
         def due(stage_at, it):
             return [rnd for rnd in range(ROUNDS) if stage_at(rnd) == it]
@@ -328,7 +335,8 @@ def tile_lstmcell_pa_t_kernel(
                 regroup_group(group - 1)
             for rnd in due(turn_at, it):
                 turn_cell(rnd)
-                copy_cell(rnd)
+                if rnd != LAST_ROUND:
+                    copy_cell(rnd)
             for rnd in due(hidden_at, it):
                 turn_output_gate(rnd)
                 form_hidden(rnd)
@@ -350,3 +358,5 @@ def tile_lstmcell_pa_t_kernel(
                     sum_cell(rnd)
             for rnd in due(squash_at, it):
                 squash_cell(rnd)
+                if rnd == LAST_ROUND:
+                    copy_cell(rnd)

@@ -327,6 +327,12 @@ def tile_lstmcell_pa_t_kernel(
         prepare(range(0, CHUNK_GROUPS), bias_stages)
         for ahead in range(GATES):
             multiply(order[ahead][0], order[ahead][1])
+
+        def pass_and_activate(it):
+            if it > 0:
+                pass_and_activate(it)
+
+        pass_and_activate(0)
         prepare(range(CHUNK_GROUPS, GROUPS), ())
 
         for it in range(0, ROUNDS + HIDDEN_LAG):

@@ -144,6 +144,13 @@ def tile_lstmcell_pa_t_kernel(
 
         bias_stages = (turn_bias, copy_bias)
 
+        zeros = consts.tile([P, CHUNK_ROWS], BF16)
+        nc.vector.memset(zeros[:], 0.0)
+
+        def keep_warm(bank, times):
+            for step in range(times):
+                nc.tensor.matmul(out=bank, lhsT=zeros[:, :P], rhs=zeros[:], start=True, stop=True)
+
         z_rows = {}
         z_turned = {}
         z_grouped = {}
@@ -227,7 +234,7 @@ def tile_lstmcell_pa_t_kernel(
 
         def turn_cell(rnd):
             if rnd == LAST_ROUND:
-                c_turned[rnd] = sum_banks.tile([P, CHUNK_GROUPS, P], F32, name="sums")
+                c_turned[rnd] = idle_banks[0][:].rearrange("p (g n) -> p g n", g=CHUNK_GROUPS)
             else:
                 c_turned[rnd] = turn_banks.tile([P, CHUNK_GROUPS, P], F32, name="c_turned", tag="turned")
             for g in range(CHUNK_GROUPS):
@@ -294,11 +301,14 @@ def tile_lstmcell_pa_t_kernel(
                     add_group(group + 1)
                 if group in groups:
                     turn_group(group)
+                    if groups.start == 0:
+                        keep_warm(idle_bank[:], 1)
                 if 0 <= group + 1 - groups.stop < len(fillers):
                     fillers[group + 1 - groups.stop]()
                 if group - 1 in groups:
                     quantise_group(group - 1)
 
+        idle_banks = []
         order = [(s, gate) for gate in range(GATES) for s in range(SLICES)]
         order.extend([(rnd, gate) for rnd in range(SLICES, ROUNDS) for gate in range(GATES)])
 
@@ -324,15 +334,12 @@ def tile_lstmcell_pa_t_kernel(
         def due(stage_at, it):
             return [rnd for rnd in range(ROUNDS) if stage_at(rnd) == it]
 
+        idle_bank = sum_banks.tile([P, CHUNK_ROWS], F32, name="sums")
+        keep_warm(idle_bank[:], 6)
         prepare(range(0, CHUNK_GROUPS), bias_stages)
         for ahead in range(GATES):
             multiply(order[ahead][0], order[ahead][1])
 
-        def pass_and_activate(it):
-            if it > 0:
-                pass_and_activate(it)
-
-        pass_and_activate(0)
         prepare(range(CHUNK_GROUPS, GROUPS), ())
 
         for it in range(0, ROUNDS + HIDDEN_LAG):
@@ -353,6 +360,10 @@ def tile_lstmcell_pa_t_kernel(
             for place in range(it * GATES, (it + 1) * GATES):
                 if place + GATES < len(order):
                     multiply(order[place + GATES][0], order[place + GATES][1])
+                elif place < len(order) - 1:
+                    idle_bank = sum_banks.tile([P, CHUNK_ROWS], F32, name="sums")
+                    keep_warm(idle_bank[:], 1)
+                    idle_banks.append(idle_bank)
                 if place < len(order):
                     activate(order[place][0], order[place][1])
             if is_group(group):

@@ -151,6 +151,11 @@ def tile_lstmcell_pa_t_kernel(
             for step in range(times):
                 nc.tensor.matmul(out=bank, lhsT=zeros[:, :P], rhs=zeros[:], start=True, stop=True)
 
+        warm = consts.tile([P, 1], F32)
+        nc.vector.memset(warm[:], 0.0)
+        warmed = consts.tile([P, 1], F32)
+        nc.scalar.activation(out=warmed[:], in_=warm[:], func=ACT.Sigmoid)
+
         z_rows = {}
         z_turned = {}
         z_grouped = {}
@@ -164,15 +169,15 @@ def tile_lstmcell_pa_t_kernel(
                 out=z_rows[group][:], in0=x_pieces[piece][:, g, :], in1=h_pieces[piece][:, g, :], op=ALU.add
             )
 
-        def turn_group(group):
+        def turn_group(group, banks=turn_banks, tag="turned"):
             words = z_rows[group][:].bitcast(F32)
-            z_turned[group] = turn_banks.tile([P, 2, GROUP_ROWS], F32, name="z_turned", tag="turned")
+            z_turned[group] = banks.tile([P, 2, GROUP_ROWS], F32, name="z_turned", tag=tag)
             for u in range(2):
                 nc.tensor.transpose(z_turned[group][:, u, :], words[:, u : FEATURES // 2 : 2], identity[:])
 
-        def regroup_group(group):
+        def regroup_group(group, copy=nc.vector.tensor_copy):
             z_grouped[group] = prep.tile([P, GROUP_ROWS * PACK], BF16, name="z_grouped", align_bytes=64)
-            nc.vector.tensor_copy(
+            copy(
                 out=z_grouped[group][:].bitcast(F32).rearrange("p (r u) -> p r u", u=2),
                 in_=z_turned[group][:].rearrange("p u r -> p r u"),
             )
@@ -277,6 +282,8 @@ def tile_lstmcell_pa_t_kernel(
 
         def turn_output_gate(rnd):
             o_turned[rnd] = turn_banks.tile([P, CHUNK_GROUPS, P], F32, name="o_turned", tag="turned")
+            if 4 <= LAST_ROUND - rnd <= 4:
+                keep_warm(o_turned[rnd][:].rearrange("p g n -> p (g n)"), 1)
             for g in range(CHUNK_GROUPS):
                 cols = slice(g * GROUP_ROWS, (g + 1) * GROUP_ROWS)
                 nc.tensor.transpose(o_turned[rnd][:, g, :], gates[rnd, OUTPUT][:, cols], identity[:])
@@ -301,8 +308,6 @@ def tile_lstmcell_pa_t_kernel(
                     add_group(group + 1)
                 if group in groups:
                     turn_group(group)
-                    if groups.start == 0:
-                        keep_warm(idle_bank[:], 1)
                 if 0 <= group + 1 - groups.stop < len(fillers):
                     fillers[group + 1 - groups.stop]()
                 if group - 1 in groups:
@@ -336,7 +341,23 @@ def tile_lstmcell_pa_t_kernel(
 
         idle_bank = sum_banks.tile([P, CHUNK_ROWS], F32, name="sums")
         keep_warm(idle_bank[:], 6)
-        prepare(range(0, CHUNK_GROUPS), bias_stages)
+        add_group(0)
+        add_group(1)
+        turn_group(0)
+        turn_group(1)
+        keep_warm(idle_bank[:], 1)
+        add_group(2)
+        add_group(3)
+        turn_group(2, sum_banks, "sums")
+        turn_group(3, sum_banks, "sums")
+        for group in range(CHUNK_GROUPS):
+            regroup_group(group, nc.scalar.copy)
+            if group == CHUNK_GROUPS - 1:
+                copy_bias()
+            quantise_group(group)
+            if group == 0:
+                turn_bias()
+                keep_warm(idle_bank[:], 2)
         for ahead in range(GATES):
             multiply(order[ahead][0], order[ahead][1])
 

@@ -73,7 +73,7 @@ def tile_lstmcell_pa_t_kernel(
         loads = stack.enter_context(tc.tile_pool(name="loads", bufs=1))
         prep = stack.enter_context(tc.tile_pool(name="prep", bufs=3))
         acts = stack.enter_context(tc.tile_pool(name="acts", bufs=SPARE))
-        results = stack.enter_context(tc.tile_pool(name="results", bufs=6))
+        results = stack.enter_context(tc.tile_pool(name="results", bufs=8))
         sum_banks = stack.enter_context(tc.psum_pool(name="sum_banks", bufs=GATES + 1))
         turn_banks = stack.enter_context(tc.psum_pool(name="turn_banks", bufs=3))
         stack.enter_context(tc.manual_schedule())
@@ -89,8 +89,8 @@ def tile_lstmcell_pa_t_kernel(
                     in_=gate_bias[gate].rearrange("(s n) -> s n", n=P),
                 )
 
-        x_pieces = []
-        h_pieces = []
+        x_pieces = {}
+        h_pieces = {}
 
         def load_piece(piece):
             rows = slice(piece * PIECE_GROUPS * GROUP_ROWS, (piece + 1) * PIECE_GROUPS * GROUP_ROWS)
@@ -98,37 +98,53 @@ def tile_lstmcell_pa_t_kernel(
             h_sb = loads.tile([P, PIECE_GROUPS, FEATURES], BF16, name="h%d" % piece)
             nc.sync.dma_start(out=x_sb[:], in_=inputs[rows, :].rearrange("(g p) k -> p g k", p=P))
             nc.sync.dma_start(out=h_sb[:], in_=short_term_memory[rows, :].rearrange("(g p) k -> p g k", p=P))
-            x_pieces.append(x_sb)
-            h_pieces.append(h_sb)
+            x_pieces[piece] = x_sb
+            h_pieces[piece] = h_sb
 
         w_words = consts.tile([P, GATES, FEATURES * PACK], U8, align_bytes=64)
         w_planes = consts.tile([P, GATES, FEATURES], U8, align_bytes=64)
         nc.vector.memset(w_planes[:].rearrange("p g n -> p (g n)").bitcast(I32), 0)
 
-        def load_gate(gate):
+        def load_scales(gate):
             for r in range(LIVE_ROWS):
                 nc.sync.dma_start(
                     out=w_planes[r:P:QUADRANT, gate, :].bitcast(I32),
                     in_=gate_scales[gate][0, r : FEATURES // QUADRANT : LIVE_ROWS, :].bitcast(I32),
                 )
+
+        def load_words(gate):
             nc.sync.dma_start(
                 out=w_words[:, gate, :].bitcast(I32),
                 in_=gate_words[gate][0].rearrange("p n t -> p (n t)").bitcast(I32),
             )
 
-        first_pieces = CHUNK_GROUPS // PIECE_GROUPS
-        load_piece(0)
-        load_biases()
-        for piece in range(1, first_pieces):
-            load_piece(piece)
-        for gate in range(GATES):
-            load_gate(gate)
-            load_piece(first_pieces + gate)
-        for piece in range(first_pieces + GATES, GROUPS // PIECE_GROUPS):
-            load_piece(piece)
-
         identity = consts.tile([P, P], F32)
         make_identity(nc, identity[:])
+        load_piece(0)
+        load_biases()
+        load_piece(1)
+        load_words(0)
+        load_scales(0)
+        load_piece(2)
+        load_words(1)
+        load_scales(1)
+        load_piece(3)
+        load_words(2)
+        load_scales(2)
+        load_words(3)
+        load_scales(3)
+        load_piece(4)
+        load_piece(5)
+        load_piece(6)
+        load_piece(7)
+        load_piece(8)
+        load_piece(9)
+        load_piece(10)
+        load_piece(11)
+        load_piece(12)
+        load_piece(13)
+        load_piece(14)
+        load_piece(15)
 
         bias_rows_f32 = consts.tile([P, P], F32)
         bias_turned = {}
@@ -336,6 +352,11 @@ def tile_lstmcell_pa_t_kernel(
             last_quantising = GROUPS - GROUP_LEAD
             return rnd + HIDDEN_LAG if rnd + HIDDEN_LAG <= last_quantising + 1 else rnd + HIDDEN_LAG - 1
 
+        def turned(it):
+            if it < SLICES - 2 or it > SLICES + 1:
+                return [it + GROUP_LEAD] if it + GROUP_LEAD < GROUPS else []
+            return ([], [8], [9], [10, 11])[it - SLICES + 2]
+
         def due(stage_at, it):
             return [rnd for rnd in range(ROUNDS) if stage_at(rnd) == it]
 
@@ -364,9 +385,8 @@ def tile_lstmcell_pa_t_kernel(
         prepare(range(CHUNK_GROUPS, GROUPS), ())
 
         for it in range(0, ROUNDS + HIDDEN_LAG):
-            group = it + GROUP_LEAD
-            if is_group(group - 1):
-                regroup_group(group - 1)
+            for group in turned(it - 1):
+                regroup_group(group)
             for rnd in due(turn_at, it):
                 turn_cell(rnd)
                 if rnd != LAST_ROUND:
@@ -374,10 +394,10 @@ def tile_lstmcell_pa_t_kernel(
             for rnd in due(hidden_at, it):
                 turn_output_gate(rnd)
                 form_hidden(rnd)
-            if is_group(group + 1):
-                add_group(group + 1)
-            if is_group(group - 1):
-                quantise_group(group - 1)
+            for group in turned(it + 1):
+                add_group(group)
+            for group in turned(it - 1):
+                quantise_group(group)
             for place in range(it * GATES, (it + 1) * GATES):
                 if place + GATES < len(order):
                     multiply(order[place + GATES][0], order[place + GATES][1])
@@ -387,7 +407,7 @@ def tile_lstmcell_pa_t_kernel(
                     idle_banks.append(idle_bank)
                 if place < len(order):
                     activate(order[place][0], order[place][1])
-            if is_group(group):
+            for group in turned(it):
                 turn_group(group)
             for rnd in due(product_at, it):
                 gate_candidate(rnd)

@@ -253,48 +253,36 @@ def tile_lstmcell_pa_t_kernel(
             cells[rnd] = acts.tile([P, CHUNK_ROWS], F32, name="cell", bufs=TURN_LAG + SPARE)
             nc.gpsimd.tensor_tensor(out=cells[rnd][:], in0=gates[rnd, FORGET][:], in1=products[rnd][:], op=ALU.add)
 
+        def turn_sum(bank, rnd, cols):
+            for summand, first in ((gates[rnd, FORGET], True), (products[rnd], False)):
+                nc.tensor.matmul(
+                    out=bank,
+                    lhsT=summand[:, cols],
+                    rhs=identity[:],
+                    start=first,
+                    stop=not first,
+                    is_transpose=True,
+                )
+
         def turn_cell(rnd):
-            if rnd == LAST_ROUND:
-                c_turned[rnd] = idle_banks[0][:].rearrange("p (g n) -> p g n", g=CHUNK_GROUPS)
-            else:
-                c_turned[rnd] = turn_banks.tile([P, CHUNK_GROUPS, P], F32, name="c_turned", tag="turned")
+            c_turned[rnd] = turn_banks.tile([P, CHUNK_GROUPS, P], F32, name="c_turned", tag="turned")
             for g in range(CHUNK_GROUPS):
                 cols = slice(g * GROUP_ROWS, (g + 1) * GROUP_ROWS)
-                if rnd in cells:
-                    nc.tensor.transpose(c_turned[rnd][:, g, :], cells[rnd][:, cols], identity[:])
-                else:
-                    nc.tensor.matmul(
-                        out=c_turned[rnd][:, g, :],
-                        lhsT=gates[rnd, FORGET][:, cols],
-                        rhs=identity[:],
-                        start=True,
-                        stop=False,
-                        is_transpose=True,
-                    )
-                    nc.tensor.matmul(
-                        out=c_turned[rnd][:, g, :],
-                        lhsT=products[rnd][:, cols],
-                        rhs=identity[:],
-                        start=False,
-                        stop=True,
-                        is_transpose=True,
-                    )
+                nc.tensor.transpose(c_turned[rnd][:, g, :], cells[rnd][:, cols], identity[:])
 
-        def store(which, rnd, rows_sb):
+        def store(which, rnd, rows_sb, groups=slice(0, CHUNK_GROUPS)):
             chunk, s = divmod(rnd, SLICES)
             block = out[which, chunk * CHUNK_ROWS : (chunk + 1) * CHUNK_ROWS, s * P : (s + 1) * P]
-            nc.sync.dma_start(out=block.rearrange("(g p) n -> p g n", p=P), in_=rows_sb[:])
+            nc.sync.dma_start(out=block.rearrange("(g p) n -> p g n", p=P)[:, groups, :], in_=rows_sb[:, groups, :])
 
         def copy_cell(rnd):
             c_rows[rnd] = results.tile([P, CHUNK_GROUPS, P], F32, name="c_rows")
-            copy = nc.scalar.copy if rnd == LAST_ROUND else nc.vector.tensor_copy
-            copy(out=c_rows[rnd][:], in_=c_turned[rnd][:])
+            nc.vector.tensor_copy(out=c_rows[rnd][:], in_=c_turned[rnd][:])
             store(0, rnd, c_rows[rnd])
 
         def squash_cell(rnd):
             tanh_c[rnd] = acts.tile([P, CHUNK_GROUPS, P], F32, name="tanh_c", bufs=HIDDEN_LAG - SQUASH_LAG + SPARE)
-            source = c_turned[rnd] if rnd == LAST_ROUND else c_rows[rnd]
-            nc.scalar.activation(out=tanh_c[rnd][:], in_=source[:], func=ACT.Tanh)
+            nc.scalar.activation(out=tanh_c[rnd][:], in_=c_rows[rnd][:], func=ACT.Tanh)
 
         def turn_output_gate(rnd):
             o_turned[rnd] = turn_banks.tile([P, CHUNK_GROUPS, P], F32, name="o_turned", tag="turned")
@@ -346,11 +334,12 @@ def tile_lstmcell_pa_t_kernel(
             return max(rnd + TURN_LAG, made_in(rnd, FORGET) + 1)
 
         def squash_at(rnd):
-            return rnd + SQUASH_LAG
+            return min(rnd + SQUASH_LAG, max(rnd + TURN_LAG, LAST_ROUND - 2))
 
         def hidden_at(rnd):
             last_quantising = GROUPS - GROUP_LEAD
-            return rnd + HIDDEN_LAG if rnd + HIDDEN_LAG <= last_quantising + 1 else rnd + HIDDEN_LAG - 1
+            lag = HIDDEN_LAG if rnd + HIDDEN_LAG <= last_quantising + 1 else HIDDEN_LAG - 1
+            return min(rnd + lag, max(rnd + 3, LAST_ROUND - 1))
 
         def turned(it):
             if it < SLICES - 2 or it > SLICES + 1:
@@ -384,13 +373,12 @@ def tile_lstmcell_pa_t_kernel(
 
         prepare(range(CHUNK_GROUPS, GROUPS), ())
 
-        for it in range(0, ROUNDS + HIDDEN_LAG):
+        for it in range(LAST_ROUND):
             for group in turned(it - 1):
                 regroup_group(group)
             for rnd in due(turn_at, it):
                 turn_cell(rnd)
-                if rnd != LAST_ROUND:
-                    copy_cell(rnd)
+                copy_cell(rnd)
             for rnd in due(hidden_at, it):
                 turn_output_gate(rnd)
                 form_hidden(rnd)
@@ -401,10 +389,6 @@ def tile_lstmcell_pa_t_kernel(
             for place in range(it * GATES, (it + 1) * GATES):
                 if place + GATES < len(order):
                     multiply(order[place + GATES][0], order[place + GATES][1])
-                elif place < len(order) - 1:
-                    idle_bank = sum_banks.tile([P, CHUNK_ROWS], F32, name="sums")
-                    keep_warm(idle_bank[:], 1)
-                    idle_banks.append(idle_bank)
                 if place < len(order):
                     activate(order[place][0], order[place][1])
             for group in turned(it):
@@ -412,9 +396,64 @@ def tile_lstmcell_pa_t_kernel(
             for rnd in due(product_at, it):
                 gate_candidate(rnd)
             for rnd in due(sum_at, it):
-                if rnd < ROUNDS - 1:
-                    sum_cell(rnd)
+                sum_cell(rnd)
             for rnd in due(squash_at, it):
                 squash_cell(rnd)
-                if rnd == LAST_ROUND:
-                    copy_cell(rnd)
+
+        def idle():
+            idle_bank = sum_banks.tile([P, CHUNK_ROWS], F32, name="sums")
+            keep_warm(idle_bank[:], 1)
+            idle_banks.append(idle_bank)
+
+        turn_cell(LAST_ROUND - 2)
+        copy_cell(LAST_ROUND - 2)
+        turn_output_gate(LAST_ROUND - 3)
+        form_hidden(LAST_ROUND - 3)
+        idle()
+        activate(LAST_ROUND, INPUT)
+        turn_cell(LAST_ROUND - 1)
+        idle()
+        activate(LAST_ROUND, CANDIDATE)
+        gate_candidate(LAST_ROUND)
+        copy_cell(LAST_ROUND - 1)
+        idle()
+        squash_cell(LAST_ROUND - 2)
+        activate(LAST_ROUND, FORGET)
+        activate(LAST_ROUND, OUTPUT)
+        squash_cell(LAST_ROUND - 1)
+        turn_output_gate(LAST_ROUND - 2)
+        turn_output_gate(LAST_ROUND - 1)
+        form_hidden(LAST_ROUND - 2)
+        halves = [slice(first, first + PIECE_GROUPS) for first in (0, PIECE_GROUPS)]
+        c_halves = []
+        for half in halves:
+            c_half = idle_banks.pop(0)
+            c_halves.append(c_half)
+            for g in range(PIECE_GROUPS):
+                cols = slice((half.start + g) * GROUP_ROWS, (half.start + g + 1) * GROUP_ROWS)
+                turn_sum(c_half[:, g * P : (g + 1) * P], LAST_ROUND, cols)
+        turn_output_gate(LAST_ROUND)
+        c_last = results.tile([P, CHUNK_GROUPS, P], F32, name="c_rows")
+        h_last = results.tile([P, CHUNK_GROUPS, P], F32, name="h_rows")
+        tanh_last = acts.tile([P, CHUNK_GROUPS, P], F32, name="tanh_c", bufs=HIDDEN_LAG - SQUASH_LAG + SPARE)
+
+        def copy_half(which):
+            nc.vector.tensor_copy(out=c_last[:, halves[which], :], in_=c_halves[which][:, : PIECE_GROUPS * P].rearrange("p (g n) -> p g n", g=PIECE_GROUPS))
+            store(0, LAST_ROUND, c_last, halves[which])
+
+        def squash_half(which):
+            nc.scalar.activation(out=tanh_last[:, halves[which], :], in_=c_halves[which][:, : PIECE_GROUPS * P].rearrange("p (g n) -> p g n", g=PIECE_GROUPS), func=ACT.Tanh)
+
+        def form_half(which):
+            nc.vector.tensor_tensor(
+                out=h_last[:, halves[which], :], in0=o_turned[LAST_ROUND][:, halves[which], :], in1=tanh_last[:, halves[which], :], op=ALU.mult
+            )
+            store(1, LAST_ROUND, h_last, halves[which])
+
+        copy_half(0)
+        squash_half(1)
+        form_hidden(LAST_ROUND - 1)
+        squash_half(0)
+        copy_half(1)
+        form_half(1)
+        form_half(0)

from contextlib import ExitStack

import concourse.mybir as mybir
from concourse.masks import make_identity

F32 = mybir.dt.float32
BF16 = mybir.dt.bfloat16
I32 = mybir.dt.int32
U32 = mybir.dt.uint32
U8 = mybir.dt.uint8
FP8X4 = mybir.dt.float8_e4m3fn_x4
ACT = mybir.ActivationFunctionType
ALU = mybir.AluOpType

P = 128
PACK = 4
QUADRANT = 32
LIVE_ROWS = 4
ROWS = 4096
FEATURES = 512
GATES = 4
INPUT = 0
CANDIDATE = 1
FORGET = 2
OUTPUT = 3
GATE_FUNC = (ACT.Sigmoid, ACT.Tanh, ACT.Sigmoid, ACT.Sigmoid)

GROUP_ROWS = P
PIECE_GROUPS = 2
CHUNK_GROUPS = 4
CHUNK_ROWS = CHUNK_GROUPS * GROUP_ROWS
CHUNKS = ROWS // CHUNK_ROWS
GROUPS = ROWS // GROUP_ROWS
SLICES = FEATURES // P
ROUNDS = CHUNKS * SLICES
LAST_ROUND = ROUNDS - 1

GROUP_LEAD = 6
TURN_LAG = 2
SQUASH_LAG = 3
HIDDEN_LAG = 5
GATE_LAG = (0, 0, TURN_LAG, HIDDEN_LAG)
SPARE = 3

FLOPS = 2 * ROWS * FEATURES * GATES * FEATURES


def tile_lstmcell_pa_t_kernel(
    tc,
    inputs,
    short_term_memory,
    Wf_words,
    Wf_scales,
    b_f,
    Wi_words,
    Wi_scales,
    b_i,
    Wg_words,
    Wg_scales,
    b_g,
    Wo_words,
    Wo_scales,
    b_o,
    out,
):
    nc = tc.nc
    gate_words = (Wi_words, Wg_words, Wf_words, Wo_words)
    gate_scales = (Wi_scales, Wg_scales, Wf_scales, Wo_scales)
    gate_bias = (b_i, b_g, b_f, b_o)

    with ExitStack() as stack:
        consts = stack.enter_context(tc.tile_pool(name="consts", bufs=1))
        loads = stack.enter_context(tc.tile_pool(name="loads", bufs=1))
        prep = stack.enter_context(tc.tile_pool(name="prep", bufs=3))
        acts = stack.enter_context(tc.tile_pool(name="acts", bufs=SPARE))
        results = stack.enter_context(tc.tile_pool(name="results", bufs=8))
        sum_banks = stack.enter_context(tc.psum_pool(name="sum_banks", bufs=GATES + 1))
        turn_banks = stack.enter_context(tc.psum_pool(name="turn_banks", bufs=3))
        stack.enter_context(tc.manual_schedule())


        bias_rows = consts.tile([P, P], BF16)
        nc.vector.memset(bias_rows[:], 0.0)

        def load_biases():
            for gate in range(GATES):
                nc.sync.dma_start(
                    out=bias_rows[gate * SLICES : (gate + 1) * SLICES, :],
                    in_=gate_bias[gate].rearrange("(s n) -> s n", n=P),
                )

        x_pieces = {}
        h_pieces = {}

        def load_piece(piece):
            rows = slice(piece * PIECE_GROUPS * GROUP_ROWS, (piece + 1) * PIECE_GROUPS * GROUP_ROWS)
            x_sb = loads.tile([P, PIECE_GROUPS, FEATURES], BF16, name="x%d" % piece)
            h_sb = loads.tile([P, PIECE_GROUPS, FEATURES], BF16, name="h%d" % piece)
            nc.sync.dma_start(out=x_sb[:], in_=inputs[rows, :].rearrange("(g p) k -> p g k", p=P))
            nc.sync.dma_start(out=h_sb[:], in_=short_term_memory[rows, :].rearrange("(g p) k -> p g k", p=P))
            x_pieces[piece] = x_sb
            h_pieces[piece] = h_sb

        w_words = consts.tile([P, GATES, FEATURES * PACK], U8, align_bytes=64)
        w_planes = consts.tile([P, GATES, FEATURES], U8, align_bytes=64)
        nc.vector.memset(w_planes[:].rearrange("p g n -> p (g n)").bitcast(I32), 0)

        def load_scales(gate):
            for r in range(LIVE_ROWS):
                nc.sync.dma_start(
                    out=w_planes[r:P:QUADRANT, gate, :].bitcast(I32),
                    in_=gate_scales[gate][0, r : FEATURES // QUADRANT : LIVE_ROWS, :].bitcast(I32),
                )

        def load_words(gate):
            nc.sync.dma_start(
                out=w_words[:, gate, :].bitcast(I32),
                in_=gate_words[gate][0].rearrange("p n t -> p (n t)").bitcast(I32),
            )

        identity = consts.tile([P, P], F32)
        make_identity(nc, identity[:])
        load_piece(0)
        load_biases()
        load_piece(1)
        load_words(0)
        load_scales(0)
        load_piece(2)
        load_words(1)
        load_scales(1)
        load_piece(3)
        load_words(2)
        load_scales(2)
        load_words(3)
        load_scales(3)
        load_piece(4)
        load_piece(5)
        load_piece(6)
        load_piece(7)
        load_piece(8)
        load_piece(9)
        load_piece(10)
        load_piece(11)
        load_piece(12)
        load_piece(13)
        load_piece(14)
        load_piece(15)

        bias_rows_f32 = consts.tile([P, P], F32)
        bias_turned = {}
        bias_cols = consts.tile([P, GATES * SLICES], F32)

        def turn_bias():
            nc.vector.tensor_copy(out=bias_rows_f32[:], in_=bias_rows[:])
            bias_turned[0] = turn_banks.tile([P, P], F32, name="bias_turned", tag="turned")
            nc.tensor.transpose(bias_turned[0][:], bias_rows_f32[:], identity[:])

        def copy_bias():
            nc.vector.tensor_copy(out=bias_cols[:], in_=bias_turned[0][:, : GATES * SLICES])

        bias_stages = (turn_bias, copy_bias)

        zeros = consts.tile([P, CHUNK_ROWS], BF16)
        nc.vector.memset(zeros[:], 0.0)

        def keep_warm(bank, times):
            for step in range(times):
                nc.tensor.matmul(out=bank, lhsT=zeros[:, :P], rhs=zeros[:], start=True, stop=True)

        warm = consts.tile([P, 1], F32)
        nc.vector.memset(warm[:], 0.0)
        warmed = consts.tile([P, 1], F32)
        nc.scalar.activation(out=warmed[:], in_=warm[:], func=ACT.Sigmoid)

        z_rows = {}
        z_turned = {}
        z_grouped = {}
        z_codes = {}
        z_planes = {}

        def add_group(group):
            piece, g = divmod(group, PIECE_GROUPS)
            z_rows[group] = prep.tile([P, FEATURES], BF16, name="z_rows")
            nc.vector.tensor_tensor(
                out=z_rows[group][:], in0=x_pieces[piece][:, g, :], in1=h_pieces[piece][:, g, :], op=ALU.add
            )

        def turn_group(group, banks=turn_banks, tag="turned"):
            words = z_rows[group][:].bitcast(F32)
            z_turned[group] = banks.tile([P, 2, GROUP_ROWS], F32, name="z_turned", tag=tag)
            for u in range(2):
                nc.tensor.transpose(z_turned[group][:, u, :], words[:, u : FEATURES // 2 : 2], identity[:])

        def regroup_group(group, copy=nc.vector.tensor_copy):
            z_grouped[group] = prep.tile([P, GROUP_ROWS * PACK], BF16, name="z_grouped", align_bytes=64)
            copy(
                out=z_grouped[group][:].bitcast(F32).rearrange("p (r u) -> p r u", u=2),
                in_=z_turned[group][:].rearrange("p u r -> p r u"),
            )

        def quantise_group(group):
            chunk, g = divmod(group, CHUNK_GROUPS)
            if g == 0:
                z_codes[chunk] = prep.tile([P, CHUNK_ROWS], U32, name="z_codes", align_bytes=64)
                z_planes[chunk] = prep.tile([P, CHUNK_ROWS], U8, name="z_planes", align_bytes=64)
            cols = slice(g * GROUP_ROWS, (g + 1) * GROUP_ROWS)
            nc.vector.quantize_mx(
                out=z_codes[chunk][:, cols].bitcast(FP8X4), scales=z_planes[chunk][:, cols], in_=z_grouped[group][:]
            )

        sums = {}
        gates = {}
        products = {}
        cells = {}
        c_turned = {}
        o_turned = {}
        tanh_c = {}
        c_rows = {}

        def multiply(rnd, gate):
            chunk, s = divmod(rnd, SLICES)
            sums[rnd, gate] = sum_banks.tile([P, CHUNK_ROWS], F32, name="sums")
            nc.tensor.matmul_mx(
                out=sums[rnd, gate][:],
                lhsT=w_words[:, gate, s * P * PACK : (s + 1) * P * PACK].bitcast(FP8X4),
                lhsT_scale=w_planes[:, gate, s * P : (s + 1) * P],
                rhs=z_codes[chunk][:].bitcast(FP8X4),
                rhs_scale=z_planes[chunk][:],
                start=True,
                stop=True,
            )

        def activate(rnd, gate):
            s = rnd % SLICES
            gates[rnd, gate] = acts.tile(
                [P, CHUNK_ROWS], F32, name="gate%d" % gate, bufs=max(GATE_LAG[gate] + SPARE, SLICES + 1)
            )
            nc.scalar.activation(
                out=gates[rnd, gate][:],
                in_=sums[rnd, gate][:],
                func=GATE_FUNC[gate],
                bias=bias_cols[:, gate * SLICES + s : gate * SLICES + s + 1],
                scale=1.0,
            )

        def gate_candidate(rnd):
            products[rnd] = acts.tile([P, CHUNK_ROWS], F32, name="product", bufs=TURN_LAG + SPARE)
            nc.vector.tensor_tensor(
                out=products[rnd][:], in0=gates[rnd, INPUT][:], in1=gates[rnd, CANDIDATE][:], op=ALU.mult
            )

        def sum_cell(rnd):
            cells[rnd] = acts.tile([P, CHUNK_ROWS], F32, name="cell", bufs=TURN_LAG + SPARE)
            nc.gpsimd.tensor_tensor(out=cells[rnd][:], in0=gates[rnd, FORGET][:], in1=products[rnd][:], op=ALU.add)

        def turn_sum(bank, rnd, cols):
            for summand, first in ((gates[rnd, FORGET], True), (products[rnd], False)):
                nc.tensor.matmul(
                    out=bank,
                    lhsT=summand[:, cols],
                    rhs=identity[:],
                    start=first,
                    stop=not first,
                    is_transpose=True,
                )

        def turn_cell(rnd):
            c_turned[rnd] = turn_banks.tile([P, CHUNK_GROUPS, P], F32, name="c_turned", tag="turned")
            for g in range(CHUNK_GROUPS):
                cols = slice(g * GROUP_ROWS, (g + 1) * GROUP_ROWS)
                nc.tensor.transpose(c_turned[rnd][:, g, :], cells[rnd][:, cols], identity[:])

        def store(which, rnd, rows_sb, groups=slice(0, CHUNK_GROUPS)):
            chunk, s = divmod(rnd, SLICES)
            block = out[which, chunk * CHUNK_ROWS : (chunk + 1) * CHUNK_ROWS, s * P : (s + 1) * P]
            nc.sync.dma_start(out=block.rearrange("(g p) n -> p g n", p=P)[:, groups, :], in_=rows_sb[:, groups, :])

        def copy_cell(rnd):
            c_rows[rnd] = results.tile([P, CHUNK_GROUPS, P], F32, name="c_rows")
            nc.vector.tensor_copy(out=c_rows[rnd][:], in_=c_turned[rnd][:])
            store(0, rnd, c_rows[rnd])

        def squash_cell(rnd):
            tanh_c[rnd] = acts.tile([P, CHUNK_GROUPS, P], F32, name="tanh_c", bufs=HIDDEN_LAG - SQUASH_LAG + SPARE)
            nc.scalar.activation(out=tanh_c[rnd][:], in_=c_rows[rnd][:], func=ACT.Tanh)

        def turn_output_gate(rnd):
            o_turned[rnd] = turn_banks.tile([P, CHUNK_GROUPS, P], F32, name="o_turned", tag="turned")
            if 4 <= LAST_ROUND - rnd <= 4:
                keep_warm(o_turned[rnd][:].rearrange("p g n -> p (g n)"), 1)
            for g in range(CHUNK_GROUPS):
                cols = slice(g * GROUP_ROWS, (g + 1) * GROUP_ROWS)
                nc.tensor.transpose(o_turned[rnd][:, g, :], gates[rnd, OUTPUT][:, cols], identity[:])

        def form_hidden(rnd):
            h_rows = results.tile([P, CHUNK_GROUPS, P], F32, name="h_rows")
            nc.vector.tensor_tensor(out=h_rows[:], in0=o_turned[rnd][:], in1=tanh_c[rnd][:], op=ALU.mult)
            store(1, rnd, h_rows)

        def is_round(rnd):
            return 0 <= rnd < ROUNDS

        def is_group(group):
            return 0 <= group < GROUPS

        def prepare(groups, fillers):
            for it in range(-GROUP_LEAD - 1, 0):
                group = it + GROUP_LEAD
                if group - 1 in groups:
                    regroup_group(group - 1)
                if group + 1 in groups:
                    add_group(group + 1)
                if group in groups:
                    turn_group(group)
                if 0 <= group + 1 - groups.stop < len(fillers):
                    fillers[group + 1 - groups.stop]()
                if group - 1 in groups:
                    quantise_group(group - 1)

        idle_banks = []
        order = [(s, gate) for gate in range(GATES) for s in range(SLICES)]
        order.extend([(rnd, gate) for rnd in range(SLICES, ROUNDS) for gate in range(GATES)])

        def made_in(rnd, gate):
            return gate if rnd < SLICES else rnd

        def product_at(rnd):
            return max(rnd, made_in(rnd, CANDIDATE))

        def sum_at(rnd):
            return max(product_at(rnd), made_in(rnd, FORGET))

        def turn_at(rnd):
            return max(rnd + TURN_LAG, made_in(rnd, FORGET) + 1)

        def squash_at(rnd):
            return min(rnd + SQUASH_LAG, max(rnd + TURN_LAG, LAST_ROUND - 2))

        def hidden_at(rnd):
            last_quantising = GROUPS - GROUP_LEAD
            lag = HIDDEN_LAG if rnd + HIDDEN_LAG <= last_quantising + 1 else HIDDEN_LAG - 1
            return min(rnd + lag, max(rnd + 3, LAST_ROUND - 1))

        def turned(it):
            if it < SLICES - 2 or it > SLICES + 1:
                return [it + GROUP_LEAD] if it + GROUP_LEAD < GROUPS else []
            return ([], [8], [9], [10, 11])[it - SLICES + 2]

        def due(stage_at, it):
            return [rnd for rnd in range(ROUNDS) if stage_at(rnd) == it]

        idle_bank = sum_banks.tile([P, CHUNK_ROWS], F32, name="sums")
        keep_warm(idle_bank[:], 6)
        add_group(0)
        add_group(1)
        turn_group(0)
        turn_group(1)
        keep_warm(idle_bank[:], 1)
        add_group(2)
        add_group(3)
        turn_group(2, sum_banks, "sums")
        turn_group(3, sum_banks, "sums")
        for group in range(CHUNK_GROUPS):
            regroup_group(group, nc.scalar.copy)
            if group == CHUNK_GROUPS - 1:
                copy_bias()
            quantise_group(group)
            if group == 0:
                turn_bias()
                keep_warm(idle_bank[:], 2)
        for ahead in range(GATES):
            multiply(order[ahead][0], order[ahead][1])

        prepare(range(CHUNK_GROUPS, GROUPS), ())

        for it in range(LAST_ROUND):
            for group in turned(it - 1):
                regroup_group(group)
            for rnd in due(turn_at, it):
                turn_cell(rnd)
                copy_cell(rnd)
            for rnd in due(hidden_at, it):
                turn_output_gate(rnd)
                form_hidden(rnd)
            for group in turned(it + 1):
                add_group(group)
            for group in turned(it - 1):
                quantise_group(group)
            for place in range(it * GATES, (it + 1) * GATES):
                if place + GATES < len(order):
                    multiply(order[place + GATES][0], order[place + GATES][1])
                if place < len(order):
                    activate(order[place][0], order[place][1])
            for group in turned(it):
                turn_group(group)
            for rnd in due(product_at, it):
                gate_candidate(rnd)
            for rnd in due(sum_at, it):
                sum_cell(rnd)
            for rnd in due(squash_at, it):
                squash_cell(rnd)

        def idle():
            idle_bank = sum_banks.tile([P, CHUNK_ROWS], F32, name="sums")
            keep_warm(idle_bank[:], 1)
            idle_banks.append(idle_bank)

        turn_cell(LAST_ROUND - 2)
        copy_cell(LAST_ROUND - 2)
        turn_output_gate(LAST_ROUND - 3)
        form_hidden(LAST_ROUND - 3)
        idle()
        activate(LAST_ROUND, INPUT)
        turn_cell(LAST_ROUND - 1)
        idle()
        activate(LAST_ROUND, CANDIDATE)
        gate_candidate(LAST_ROUND)
        copy_cell(LAST_ROUND - 1)
        idle()
        squash_cell(LAST_ROUND - 2)
        activate(LAST_ROUND, FORGET)
        activate(LAST_ROUND, OUTPUT)
        squash_cell(LAST_ROUND - 1)
        turn_output_gate(LAST_ROUND - 2)
        turn_output_gate(LAST_ROUND - 1)
        form_hidden(LAST_ROUND - 2)
        halves = [slice(first, first + PIECE_GROUPS) for first in (0, PIECE_GROUPS)]
        c_halves = []
        for half in halves:
            c_half = idle_banks.pop(0)
            c_halves.append(c_half)
            for g in range(PIECE_GROUPS):
                cols = slice((half.start + g) * GROUP_ROWS, (half.start + g + 1) * GROUP_ROWS)
                turn_sum(c_half[:, g * P : (g + 1) * P], LAST_ROUND, cols)
        turn_output_gate(LAST_ROUND)
        c_last = results.tile([P, CHUNK_GROUPS, P], F32, name="c_rows")
        h_last = results.tile([P, CHUNK_GROUPS, P], F32, name="h_rows")
        tanh_last = acts.tile([P, CHUNK_GROUPS, P], F32, name="tanh_c", bufs=HIDDEN_LAG - SQUASH_LAG + SPARE)

        def copy_half(which):
            nc.vector.tensor_copy(out=c_last[:, halves[which], :], in_=c_halves[which][:, : PIECE_GROUPS * P].rearrange("p (g n) -> p g n", g=PIECE_GROUPS))
            store(0, LAST_ROUND, c_last, halves[which])

        def squash_half(which):
            nc.scalar.activation(out=tanh_last[:, halves[which], :], in_=c_halves[which][:, : PIECE_GROUPS * P].rearrange("p (g n) -> p g n", g=PIECE_GROUPS), func=ACT.Tanh)

        def form_half(which):
            nc.vector.tensor_tensor(
                out=h_last[:, halves[which], :], in0=o_turned[LAST_ROUND][:, halves[which], :], in1=tanh_last[:, halves[which], :], op=ALU.mult
            )
            store(1, LAST_ROUND, h_last, halves[which])

        copy_half(0)
        squash_half(1)
        form_hidden(LAST_ROUND - 1)
        squash_half(0)
        copy_half(1)
        form_half(1)
        form_half(0)
